import numpy as np
import ml_dtypes


def mxq(x, axis, fmt="e4m3"):
    dtype, down = {"e4m3": (ml_dtypes.float8_e4m3fn, 7), "e5m2": (ml_dtypes.float8_e5m2, 14)}[fmt]
    v = np.moveaxis(np.asarray(x, np.float32).astype(ml_dtypes.bfloat16).astype(np.float64), axis, -1)
    blocks = v.reshape(v.shape[:-1] + (-1, 32))
    amax = np.abs(blocks).max(-1, keepdims=True)
    byte = np.maximum(np.where(amax > 0, np.frexp(amax)[1] - 1 + 127, 0) - down, 1)
    scale = np.exp2(byte - 127.0)
    codes = (blocks / scale).astype(np.float32).astype(dtype).astype(np.float64)
    return np.moveaxis((codes * scale).reshape(v.shape), -1, axis)


WIDE = False


def mx_kscale(k):
    if not WIDE:
        return np.ones(k)
    levels = np.array([10, -10, 5, -5, 0])
    a = np.random.permutation(np.resize(levels, k // 512 * 4)).reshape(k // 512, 4)
    idx = np.arange(k)
    return np.exp2(a[idx // 512, idx % 128 // 32])


BF16 = ml_dtypes.bfloat16


def bf(x):
    return np.asarray(x, np.float32).astype(BF16)


def f64(x):
    return np.asarray(x).astype(np.float64)


B, L, LV, H = 4, 32, 64, 1024
NUM_ITERATIONS = 3
X = 0.25
V = 0.12 * L
A = 0.6 / (np.sqrt(H) * V)


def setup_inputs():
    s = mx_kscale(H)
    return {"text_feat": bf(np.random.standard_normal((B, L, H)) * X * s),
            "vision_proj": bf(np.random.standard_normal((B, 1, H)) * V),
            "Wt": bf(np.random.standard_normal((H, H)) * A / (X * np.sqrt(H)) / s[None, :]),
            "bt": bf(np.random.standard_normal(H) * 0.5 * A)}


def reference(text_feat, vision_proj, Wt, bt):
    vp = f64(vision_proj)
    text_proj = (mxq(f64(text_feat), 2, "e4m3") @ mxq(f64(Wt), 1, "e4m3").T) + f64(bt)
    agreement = np.sum(text_proj * vp, axis=-1, keepdims=True)
    coupling = np.zeros_like(agreement)
    for _ in range(NUM_ITERATIONS - 1):
        coupling = coupling + agreement
    e = np.exp(coupling - coupling.max(axis=1, keepdims=True))
    routing_weights = e / e.sum(axis=1, keepdims=True)
    weighted_vision = routing_weights * vp
    return text_proj, weighted_vision

@@ -1,0 +1,161 @@
+from contextlib import ExitStack
+
+import concourse.masks as masks
+import concourse.mybir as mybir
+
+F32 = mybir.dt.float32
+BF16 = mybir.dt.bfloat16
+U32 = mybir.dt.uint32
+U8 = mybir.dt.uint8
+FP8X4 = mybir.dt.float8_e4m3fn_x4
+ALU = mybir.AluOpType
+ACT = mybir.ActivationFunctionType
+AXIS = mybir.AxisListType
+
+P = 128
+BATCH = 4
+TOKENS = 32
+K = 1024
+H = 1024
+PACK = 4
+K_PASS = P * PACK
+PASSES = K // K_PASS
+WORDS = K // 2
+FLIPS = WORDS // P
+BLOCKS = H // P
+COUPLING_ROUNDS = 2.0
+LAG = 2
+HALF = H // 2
+
+FLOPS = 2 * P * K * H
+
+
+def tile_dynamicroutingfusion_pa_s_kernel(tc, text_feat, vision_proj, Wt, bt, out_0, out_1):
+    nc = tc.nc
+    text_rows = text_feat.rearrange("b l k -> (b l) k")
+    text_proj_out = out_0.rearrange("b l h -> (b l) h")
+    weighted_out = out_1.rearrange("b l h -> (b l) h")
+
+    with ExitStack() as ctx:
+        keep = ctx.enter_context(tc.tile_pool(name="keep", bufs=1))
+        stage = ctx.enter_context(tc.tile_pool(name="stage", bufs=3))
+        flip_banks = ctx.enter_context(tc.psum_pool(name="flip_banks", bufs=4))
+        sum_banks = ctx.enter_context(tc.psum_pool(name="sum_banks", bufs=4))
+
+        x_rows = keep.tile([P, K], BF16)
+        nc.sync.dma_start(out=x_rows[:], in_=text_rows)
+        w_rows = keep.tile([P, BLOCKS, K], BF16)
+        for r in range(BLOCKS):
+            nc.sync.dma_start(out=w_rows[:, r, :], in_=Wt[r * P : (r + 1) * P, :])
+        bias_rows = keep.tile([P, H], BF16)
+        nc.scalar.dma_start(out=bias_rows[:], in_=bt.partition_broadcast(P))
+        vision_rows = keep.tile([P, H], BF16)
+        for b in range(BATCH):
+            nc.scalar.dma_start(
+                out=vision_rows[b * TOKENS : (b + 1) * TOKENS, :],
+                in_=vision_proj[b, 0, :].partition_broadcast(TOKENS),
+            )
+
+        identity = keep.tile([P, P], F32)
+        masks.make_identity(nc, identity[:])
+        table_warmer = keep.tile([P, 1], F32)
+        nc.vector.memset(table_warmer[:], 0.0)
+        nc.scalar.activation(out=table_warmer[:], in_=table_warmer[:], func=ACT.Exp)
+
+        x_codes = keep.tile([P, PASSES * P], U32, align_bytes=64)
+        x_scales = keep.tile([P, PASSES * P], U8, align_bytes=64)
+        w_codes = keep.tile([P, BLOCKS, PASSES * P], U32, align_bytes=64)
+        w_scales = keep.tile([P, BLOCKS, PASSES * P], U8, align_bytes=64)
+
+        def flip(rows):
+            words = rows.bitcast(F32)
+            bank = flip_banks.tile([P, FLIPS, P], F32)
+            for j in range(FLIPS):
+                nc.tensor.transpose(bank[:, j, :], words[:, j * P : (j + 1) * P], identity[:])
+            grouped = stage.tile([P, PASSES * P * PACK], BF16, align_bytes=64)
+            nc.scalar.copy(
+                out=grouped[:].bitcast(F32).rearrange("p (g r u) -> p g r u", g=PASSES, u=2),
+                in_=bank[:].rearrange("p (g u) r -> p g r u", u=2),
+            )
+            return grouped
+
+        def quantise(grouped, codes, scales):
+            nc.vector.quantize_mx(out=codes.bitcast(FP8X4), scales=scales, in_=grouped[:])
+
+        text_proj = keep.tile([P, H], F32)
+        products = keep.tile([P, H], F32)
+        coupling_parts = keep.tile([P, BLOCKS], F32)
+
+        def multiply(r):
+            sums = sum_banks.tile([P, P], F32)
+            for g in range(PASSES):
+                cols = slice(g * P, (g + 1) * P)
+                nc.tensor.matmul_mx(
+                    out=sums[:],
+                    lhsT=x_codes[:, cols].bitcast(FP8X4),
+                    lhsT_scale=x_scales[:, cols],
+                    rhs=w_codes[:, r, cols].bitcast(FP8X4),
+                    rhs_scale=w_scales[:, r, cols],
+                    start=(g == 0),
+                    stop=(g == PASSES - 1),
+                )
+            h_cols = slice(r * P, (r + 1) * P)
+            nc.vector.scalar_tensor_tensor(
+                out=products[:, h_cols],
+                in0=sums[:],
+                scalar=COUPLING_ROUNDS,
+                in1=vision_rows[:, h_cols],
+                op0=ALU.mult,
+                op1=ALU.mult,
+                accum_out=coupling_parts[:, r : r + 1],
+            )
+            nc.vector.tensor_tensor(
+                out=text_proj[:, h_cols], in0=sums[:], in1=bias_rows[:, h_cols], op=ALU.add
+            )
+
+        quantise(flip(x_rows[:]), x_codes[:], x_scales[:])
+        flipped = {}
+        for step in range(BLOCKS + LAG):
+            if step < BLOCKS:
+                flipped[step] = flip(w_rows[:, step, :])
+            if 1 <= step <= BLOCKS:
+                quantise(flipped[step - 1], w_codes[:, step - 1, :], w_scales[:, step - 1, :])
+            if step >= LAG:
+                multiply(step - LAG)
+            if step - LAG == BLOCKS // 2 - 1:
+                nc.sync.dma_start(out=text_proj_out[:, :HALF], in_=text_proj[:, :HALF])
+        nc.sync.dma_start(out=text_proj_out[:, HALF:], in_=text_proj[:, HALF:])
+
+        own_coupling = keep.tile([P, TOKENS], F32, align_bytes=64)
+        nc.vector.tensor_reduce(
+            out=own_coupling[:],
+            in_=coupling_parts[:].unsqueeze(1).to_broadcast([P, TOKENS, BLOCKS]),
+            axis=AXIS.X,
+            op=ALU.add,
+        )
+        group_coupling = keep.tile([P, TOKENS], F32, align_bytes=64)
+        nc.vector.transpose(out=group_coupling[:], in_=own_coupling[:])
+        minus_max = keep.tile([P, 1], F32)
+        nc.vector.tensor_reduce(
+            out=minus_max[:], in_=group_coupling[:], axis=AXIS.X, op=ALU.max, negate=True
+        )
+        group_exp = keep.tile([P, TOKENS], F32)
+        exp_sum = keep.tile([P, 1], F32)
+        nc.scalar.activation(
+            out=group_exp[:], in_=group_coupling[:], func=ACT.Exp, bias=minus_max[:], accum_out=exp_sum[:]
+        )
+        own_exp = keep.tile([P, 1], F32)
+        nc.scalar.activation(out=own_exp[:], in_=own_coupling[:, 0:1], func=ACT.Exp, bias=minus_max[:])
+        one_over_sum = keep.tile([P, 1], F32)
+        nc.vector.reciprocal(out=one_over_sum[:], in_=exp_sum[:])
+        routing = keep.tile([P, 1], F32)
+        nc.vector.tensor_tensor(out=routing[:], in0=own_exp[:], in1=one_over_sum[:], op=ALU.mult)
+
+        weighted_left = keep.tile([P, HALF], F32)
+        nc.vector.tensor_scalar(
+            out=weighted_left[:], in0=vision_rows[:, :HALF], scalar1=routing[:], scalar2=None, op0=ALU.mult
+        )
+        nc.sync.dma_start(out=weighted_out[:, :HALF], in_=weighted_left[:])
+        weighted_right = keep.tile([P, HALF], F32)
+        nc.scalar.activation(out=weighted_right[:], in_=vision_rows[:, HALF:], func=ACT.Copy, scale=routing[:])
+        nc.scalar.dma_start(out=weighted_out[:, HALF:], in_=weighted_right[:])

@@ -43,18 +43,28 @@ def tile_dynamicroutingfusion_pa_s_kernel(tc, text_feat, vision_proj, Wt, bt, ou
         sum_banks = ctx.enter_context(tc.psum_pool(name="sum_banks", bufs=4))
 
         x_rows = keep.tile([P, K], BF16)
-        nc.sync.dma_start(out=x_rows[:], in_=text_rows)
         w_rows = keep.tile([P, BLOCKS, K], BF16)
-        for r in range(BLOCKS):
-            nc.sync.dma_start(out=w_rows[:, r, :], in_=Wt[r * P : (r + 1) * P, :])
         bias_rows = keep.tile([P, H], BF16)
-        nc.scalar.dma_start(out=bias_rows[:], in_=bt.partition_broadcast(P))
         vision_rows = keep.tile([P, H], BF16)
+
+        def load_blocks(first, count):
+            nc.sync.dma_start(
+                out=w_rows[:, first : first + count, :],
+                in_=Wt[first * P : (first + count) * P, :].rearrange("(j p) k -> p j k", p=P),
+            )
+
+        nc.sync.dma_start(out=x_rows[:], in_=text_rows)
+        load_blocks(0, 2)
+        nc.sync.dma_start(out=bias_rows[:], in_=bt.partition_broadcast(P))
         for b in range(BATCH):
-            nc.scalar.dma_start(
+            nc.sync.dma_start(
                 out=vision_rows[b * TOKENS : (b + 1) * TOKENS, :],
                 in_=vision_proj[b, 0, :].partition_broadcast(TOKENS),
             )
+        for first in range(2, BLOCKS - 2, 2):
+            load_blocks(first, 2)
+        load_blocks(BLOCKS - 2, 1)
+        load_blocks(BLOCKS - 1, 1)
 
         identity = keep.tile([P, P], F32)
         masks.make_identity(nc, identity[:])

@@ -26,6 +26,7 @@ BLOCKS = H // P
 COUPLING_ROUNDS = 2.0
 LAG = 2
 HALF = H // 2
+WARM_PASSES = 20
 
 FLOPS = 2 * P * K * H
 
@@ -71,6 +72,23 @@ def tile_dynamicroutingfusion_pa_s_kernel(tc, text_feat, vision_proj, Wt, bt, ou
         table_warmer = keep.tile([P, 1], F32)
         nc.vector.memset(table_warmer[:], 0.0)
         nc.scalar.activation(out=table_warmer[:], in_=table_warmer[:], func=ACT.Exp)
+
+        zeros = keep.tile([P, P * PACK], BF16, align_bytes=64)
+        zero_codes = keep.tile([P, P], U32, align_bytes=64)
+        zero_scales = keep.tile([P, P], U8, align_bytes=64)
+        nc.vector.memset(zeros[:], 0.0)
+        nc.vector.quantize_mx(out=zero_codes[:].bitcast(FP8X4), scales=zero_scales[:], in_=zeros[:])
+        bank = flip_banks.tile([P, FLIPS, P], F32)
+        for warm_pass in range(WARM_PASSES):
+            nc.tensor.matmul_mx(
+                out=bank[:, 0, :],
+                lhsT=zero_codes[:].bitcast(FP8X4),
+                lhsT_scale=zero_scales[:],
+                rhs=zero_codes[:].bitcast(FP8X4),
+                rhs_scale=zero_scales[:],
+                start=True,
+                stop=True,
+            )
 
         x_codes = keep.tile([P, PASSES * P], U32, align_bytes=64)
         x_scales = keep.tile([P, PASSES * P], U8, align_bytes=64)

@@ -26,7 +26,8 @@ BLOCKS = H // P
 COUPLING_ROUNDS = 2.0
 LAG = 2
 HALF = H // 2
-WARM_PASSES = 20
+SQUARE = 32
+CHUNK = H // SQUARE
 
 FLOPS = 2 * P * K * H
 
@@ -45,8 +46,7 @@ def tile_dynamicroutingfusion_pa_s_kernel(tc, text_feat, vision_proj, Wt, bt, ou
 
         x_rows = keep.tile([P, K], BF16)
         w_rows = keep.tile([P, BLOCKS, K], BF16)
-        bias_rows = keep.tile([P, H], BF16)
-        vision_rows = keep.tile([P, H], BF16)
+        seed = keep.tile([P, 2, CHUNK], BF16, align_bytes=64)
 
         def load_blocks(first, count):
             nc.sync.dma_start(
@@ -54,15 +54,13 @@ def tile_dynamicroutingfusion_pa_s_kernel(tc, text_feat, vision_proj, Wt, bt, ou
                 in_=Wt[first * P : (first + count) * P, :].rearrange("(j p) k -> p j k", p=P),
             )
 
-        nc.sync.dma_start(out=x_rows[:], in_=text_rows)
-        load_blocks(0, 2)
-        nc.sync.dma_start(out=bias_rows[:], in_=bt.partition_broadcast(P))
+        nc.scalar.dma_start(out=seed[:, 0, :], in_=vision_proj.rearrange("b o (m e) -> (b o m) e", e=CHUNK))
         for b in range(BATCH):
-            nc.sync.dma_start(
-                out=vision_rows[b * TOKENS : (b + 1) * TOKENS, :],
-                in_=vision_proj[b, 0, :].partition_broadcast(TOKENS),
+            nc.scalar.dma_start(
+                out=seed[b * SQUARE : (b + 1) * SQUARE, 1, :], in_=bt.rearrange("(m e) -> m e", e=CHUNK)
             )
-        for first in range(2, BLOCKS - 2, 2):
+        nc.sync.dma_start(out=x_rows[:], in_=text_rows)
+        for first in range(0, BLOCKS - 2, 2):
             load_blocks(first, 2)
         load_blocks(BLOCKS - 2, 1)
         load_blocks(BLOCKS - 1, 1)
@@ -73,22 +71,22 @@ def tile_dynamicroutingfusion_pa_s_kernel(tc, text_feat, vision_proj, Wt, bt, ou
         nc.vector.memset(table_warmer[:], 0.0)
         nc.scalar.activation(out=table_warmer[:], in_=table_warmer[:], func=ACT.Exp)
 
-        zeros = keep.tile([P, P * PACK], BF16, align_bytes=64)
-        zero_codes = keep.tile([P, P], U32, align_bytes=64)
-        zero_scales = keep.tile([P, P], U8, align_bytes=64)
-        nc.vector.memset(zeros[:], 0.0)
-        nc.vector.quantize_mx(out=zero_codes[:].bitcast(FP8X4), scales=zero_scales[:], in_=zeros[:])
-        bank = flip_banks.tile([P, FLIPS, P], F32)
-        for warm_pass in range(WARM_PASSES):
-            nc.tensor.matmul_mx(
-                out=bank[:, 0, :],
-                lhsT=zero_codes[:].bitcast(FP8X4),
-                lhsT_scale=zero_scales[:],
-                rhs=zero_codes[:].bitcast(FP8X4),
-                rhs_scale=zero_scales[:],
-                start=True,
-                stop=True,
-            )
+        seed_flipped = keep.tile([P, SQUARE], F32, align_bytes=64)
+        nc.vector.transpose(out=seed_flipped[:], in_=seed[:].rearrange("p w e -> p (w e)").bitcast(F32))
+        seed_repeated = keep.tile([P, SQUARE, SQUARE], F32, align_bytes=64)
+        nc.vector.tensor_copy(
+            out=seed_repeated[:], in_=seed_flipped[:].unsqueeze(2).to_broadcast([P, SQUARE, SQUARE])
+        )
+        both_rows = keep.tile([P, SQUARE, 2, CHUNK], BF16, align_bytes=64)
+        nc.vector.transpose(
+            out=both_rows[:].rearrange("p m w e -> p (m w e)").bitcast(F32),
+            in_=seed_repeated[:].rearrange("p m i -> p (m i)"),
+        )
+        vision_rows = both_rows[:, :, 0, :]
+        bias_rows = both_rows[:, :, 1, :]
+
+        def chunked(columns):
+            return columns.rearrange("p (m e) -> p m e", e=CHUNK)
 
         x_codes = keep.tile([P, PASSES * P], U32, align_bytes=64)
         x_scales = keep.tile([P, PASSES * P], U8, align_bytes=64)
@@ -128,17 +126,18 @@ def tile_dynamicroutingfusion_pa_s_kernel(tc, text_feat, vision_proj, Wt, bt, ou
                     stop=(g == PASSES - 1),
                 )
             h_cols = slice(r * P, (r + 1) * P)
+            m_rows = slice(r * P // CHUNK, (r + 1) * P // CHUNK)
             nc.vector.scalar_tensor_tensor(
-                out=products[:, h_cols],
-                in0=sums[:],
+                out=chunked(products[:, h_cols]),
+                in0=chunked(sums[:]),
                 scalar=COUPLING_ROUNDS,
-                in1=vision_rows[:, h_cols],
+                in1=vision_rows[:, m_rows, :],
                 op0=ALU.mult,
                 op1=ALU.mult,
                 accum_out=coupling_parts[:, r : r + 1],
             )
             nc.vector.tensor_tensor(
-                out=text_proj[:, h_cols], in0=sums[:], in1=bias_rows[:, h_cols], op=ALU.add
+                out=chunked(text_proj[:, h_cols]), in0=chunked(sums[:]), in1=bias_rows[:, m_rows, :], op=ALU.add
             )
 
         quantise(flip(x_rows[:]), x_codes[:], x_scales[:])
@@ -181,9 +180,15 @@ def tile_dynamicroutingfusion_pa_s_kernel(tc, text_feat, vision_proj, Wt, bt, ou
 
         weighted_left = keep.tile([P, HALF], F32)
         nc.vector.tensor_scalar(
-            out=weighted_left[:], in0=vision_rows[:, :HALF], scalar1=routing[:], scalar2=None, op0=ALU.mult
+            out=chunked(weighted_left[:]),
+            in0=vision_rows[:, : HALF // CHUNK, :],
+            scalar1=routing[:],
+            scalar2=None,
+            op0=ALU.mult,
         )
         nc.sync.dma_start(out=weighted_out[:, :HALF], in_=weighted_left[:])
         weighted_right = keep.tile([P, HALF], F32)
-        nc.scalar.activation(out=weighted_right[:], in_=vision_rows[:, HALF:], func=ACT.Copy, scale=routing[:])
+        nc.scalar.activation(
+            out=chunked(weighted_right[:]), in_=vision_rows[:, HALF // CHUNK :, :], func=ACT.Copy, scale=routing[:]
+        )
         nc.scalar.dma_start(out=weighted_out[:, HALF:], in_=weighted_right[:])

@@ -23,8 +23,9 @@ PASSES = K // K_PASS
 WORDS = K // 2
 FLIPS = WORDS // P
 BLOCKS = H // P
+RUN = 2
+RUNS = BLOCKS // RUN
 COUPLING_ROUNDS = 2.0
-LAG = 2
 HALF = H // 2
 SQUARE = 32
 CHUNK = H // SQUARE
@@ -39,8 +40,9 @@ def tile_dynamicroutingfusion_pa_s_kernel(tc, text_feat, vision_proj, Wt, bt, ou
     weighted_out = out_1.rearrange("b l h -> (b l) h")
 
     with ExitStack() as ctx:
+        ctx.enter_context(tc.manual_schedule())
         keep = ctx.enter_context(tc.tile_pool(name="keep", bufs=1))
-        stage = ctx.enter_context(tc.tile_pool(name="stage", bufs=3))
+        stage = ctx.enter_context(tc.tile_pool(name="stage", bufs=2 * RUN))
         flip_banks = ctx.enter_context(tc.psum_pool(name="flip_banks", bufs=4))
         sum_banks = ctx.enter_context(tc.psum_pool(name="sum_banks", bufs=4))
 
@@ -125,33 +127,42 @@ def tile_dynamicroutingfusion_pa_s_kernel(tc, text_feat, vision_proj, Wt, bt, ou
                     start=(g == 0),
                     stop=(g == PASSES - 1),
                 )
-            h_cols = slice(r * P, (r + 1) * P)
-            m_rows = slice(r * P // CHUNK, (r + 1) * P // CHUNK)
             nc.vector.scalar_tensor_tensor(
-                out=chunked(products[:, h_cols]),
+                out=chunked(products[:, r * P : (r + 1) * P]),
                 in0=chunked(sums[:]),
                 scalar=COUPLING_ROUNDS,
-                in1=vision_rows[:, m_rows, :],
+                in1=vision_rows[:, r * P // CHUNK : (r + 1) * P // CHUNK, :],
                 op0=ALU.mult,
                 op1=ALU.mult,
                 accum_out=coupling_parts[:, r : r + 1],
             )
+            return sums
+
+        def add_bias(r, sums):
             nc.vector.tensor_tensor(
-                out=chunked(text_proj[:, h_cols]), in0=chunked(sums[:]), in1=bias_rows[:, m_rows, :], op=ALU.add
+                out=chunked(text_proj[:, r * P : (r + 1) * P]),
+                in0=chunked(sums[:]),
+                in1=bias_rows[:, r * P // CHUNK : (r + 1) * P // CHUNK, :],
+                op=ALU.add,
             )
 
         quantise(flip(x_rows[:]), x_codes[:], x_scales[:])
-        flipped = {}
-        for step in range(BLOCKS + LAG):
-            if step < BLOCKS:
-                flipped[step] = flip(w_rows[:, step, :])
-            if 1 <= step <= BLOCKS:
-                quantise(flipped[step - 1], w_codes[:, step - 1, :], w_scales[:, step - 1, :])
-            if step >= LAG:
-                multiply(step - LAG)
-            if step - LAG == BLOCKS // 2 - 1:
+        last_sums = []
+        for run in range(RUNS + 1):
+            if run < RUNS:
+                blocks = range(run * RUN, (run + 1) * RUN)
+                flipped = [flip(w_rows[:, r, :]) for r in blocks]
+                for r, grouped in zip(blocks, flipped):
+                    quantise(grouped, w_codes[:, r, :], w_scales[:, r, :])
+            if run >= 1:
+                for r in range((run - 1) * RUN, run * RUN):
+                    sums = multiply(r)
+                    if run < RUNS:
+                        add_bias(r, sums)
+                    else:
+                        last_sums.append((r, sums))
+            if run * RUN == BLOCKS // 2:
                 nc.sync.dma_start(out=text_proj_out[:, :HALF], in_=text_proj[:, :HALF])
-        nc.sync.dma_start(out=text_proj_out[:, HALF:], in_=text_proj[:, HALF:])
 
         own_coupling = keep.tile([P, TOKENS], F32, align_bytes=64)
         nc.vector.tensor_reduce(
@@ -173,6 +184,9 @@ def tile_dynamicroutingfusion_pa_s_kernel(tc, text_feat, vision_proj, Wt, bt, ou
         )
         own_exp = keep.tile([P, 1], F32)
         nc.scalar.activation(out=own_exp[:], in_=own_coupling[:, 0:1], func=ACT.Exp, bias=minus_max[:])
+        for r, sums in last_sums:
+            add_bias(r, sums)
+        nc.sync.dma_start(out=text_proj_out[:, HALF:], in_=text_proj[:, HALF:])
         one_over_sum = keep.tile([P, 1], F32)
         nc.vector.reciprocal(out=one_over_sum[:], in_=exp_sum[:])
         routing = keep.tile([P, 1], F32)

@@ -29,6 +29,8 @@ COUPLING_ROUNDS = 2.0
 HALF = H // 2
 SQUARE = 32
 CHUNK = H // SQUARE
+IDLE_COLUMNS = 512
+IDLE_PASSES = 3
 
 FLOPS = 2 * P * K * H
 
@@ -73,6 +75,25 @@ def tile_dynamicroutingfusion_pa_s_kernel(tc, text_feat, vision_proj, Wt, bt, ou
         nc.vector.memset(table_warmer[:], 0.0)
         nc.scalar.activation(out=table_warmer[:], in_=table_warmer[:], func=ACT.Exp)
 
+        zeros = keep.tile([P, IDLE_COLUMNS * PACK], BF16, align_bytes=64)
+        zero_codes = keep.tile([P, IDLE_COLUMNS], U32, align_bytes=64)
+        zero_scales = keep.tile([P, IDLE_COLUMNS], U8, align_bytes=64)
+        nc.vector.memset(zeros[:], 0.0)
+        nc.vector.quantize_mx(out=zero_codes[:].bitcast(FP8X4), scales=zero_scales[:], in_=zeros[:])
+
+        def idle_passes():
+            unread = sum_banks.tile([P, IDLE_COLUMNS], F32, tag="sum_bank")
+            for idle_pass in range(IDLE_PASSES):
+                nc.tensor.matmul_mx(
+                    out=unread[:],
+                    lhsT=zero_codes[:, :P].bitcast(FP8X4),
+                    lhsT_scale=zero_scales[:, :P],
+                    rhs=zero_codes[:].bitcast(FP8X4),
+                    rhs_scale=zero_scales[:],
+                    start=True,
+                    stop=True,
+                )
+
         seed_flipped = keep.tile([P, SQUARE], F32, align_bytes=64)
         nc.vector.transpose(out=seed_flipped[:], in_=seed[:].rearrange("p w e -> p (w e)").bitcast(F32))
         seed_repeated = keep.tile([P, SQUARE, SQUARE], F32, align_bytes=64)
@@ -115,7 +136,7 @@ def tile_dynamicroutingfusion_pa_s_kernel(tc, text_feat, vision_proj, Wt, bt, ou
         coupling_parts = keep.tile([P, BLOCKS], F32)
 
         def multiply(r):
-            sums = sum_banks.tile([P, P], F32)
+            sums = sum_banks.tile([P, P], F32, tag="sum_bank")
             for g in range(PASSES):
                 cols = slice(g * P, (g + 1) * P)
                 nc.tensor.matmul_mx(
@@ -146,7 +167,9 @@ def tile_dynamicroutingfusion_pa_s_kernel(tc, text_feat, vision_proj, Wt, bt, ou
                 op=ALU.add,
             )
 
+        idle_passes()
         quantise(flip(x_rows[:]), x_codes[:], x_scales[:])
+        idle_passes()
         last_sums = []
         for run in range(RUNS + 1):
             if run < RUNS:
@@ -154,6 +177,8 @@ def tile_dynamicroutingfusion_pa_s_kernel(tc, text_feat, vision_proj, Wt, bt, ou
                 flipped = [flip(w_rows[:, r, :]) for r in blocks]
                 for r, grouped in zip(blocks, flipped):
                     quantise(grouped, w_codes[:, r, :], w_scales[:, r, :])
+            if run == 0:
+                idle_passes()
             if run >= 1:
                 for r in range((run - 1) * RUN, run * RUN):
                     sums = multiply(r)

@@ -7,6 +7,7 @@ F32 = mybir.dt.float32
 BF16 = mybir.dt.bfloat16
 U32 = mybir.dt.uint32
 U8 = mybir.dt.uint8
+I32 = mybir.dt.int32
 FP8X4 = mybir.dt.float8_e4m3fn_x4
 ALU = mybir.AluOpType
 ACT = mybir.ActivationFunctionType
@@ -29,8 +30,10 @@ COUPLING_ROUNDS = 2.0
 HALF = H // 2
 SQUARE = 32
 CHUNK = H // SQUARE
-IDLE_COLUMNS = 512
-IDLE_PASSES = 3
+IDLE_COLUMNS = 256
+IDLE_START = 10
+IDLE_HOLD = 3
+LATE_ADDS = 2
 
 FLOPS = 2 * P * K * H
 
@@ -78,12 +81,12 @@ def tile_dynamicroutingfusion_pa_s_kernel(tc, text_feat, vision_proj, Wt, bt, ou
         zeros = keep.tile([P, IDLE_COLUMNS * PACK], BF16, align_bytes=64)
         zero_codes = keep.tile([P, IDLE_COLUMNS], U32, align_bytes=64)
         zero_scales = keep.tile([P, IDLE_COLUMNS], U8, align_bytes=64)
-        nc.vector.memset(zeros[:], 0.0)
+        nc.vector.memset(zeros[:].bitcast(I32), 0)
         nc.vector.quantize_mx(out=zero_codes[:].bitcast(FP8X4), scales=zero_scales[:], in_=zeros[:])
 
-        def idle_passes():
+        def idle_passes(count):
             unread = sum_banks.tile([P, IDLE_COLUMNS], F32, tag="sum_bank")
-            for idle_pass in range(IDLE_PASSES):
+            for idle_pass in range(count):
                 nc.tensor.matmul_mx(
                     out=unread[:],
                     lhsT=zero_codes[:, :P].bitcast(FP8X4),
@@ -167,9 +170,9 @@ def tile_dynamicroutingfusion_pa_s_kernel(tc, text_feat, vision_proj, Wt, bt, ou
                 op=ALU.add,
             )
 
-        idle_passes()
+        idle_passes(IDLE_START)
         quantise(flip(x_rows[:]), x_codes[:], x_scales[:])
-        idle_passes()
+        idle_passes(IDLE_HOLD)
         last_sums = []
         for run in range(RUNS + 1):
             if run < RUNS:
@@ -178,11 +181,11 @@ def tile_dynamicroutingfusion_pa_s_kernel(tc, text_feat, vision_proj, Wt, bt, ou
                 for r, grouped in zip(blocks, flipped):
                     quantise(grouped, w_codes[:, r, :], w_scales[:, r, :])
             if run == 0:
-                idle_passes()
+                idle_passes(IDLE_HOLD)
             if run >= 1:
                 for r in range((run - 1) * RUN, run * RUN):
                     sums = multiply(r)
-                    if run < RUNS:
+                    if run <= RUNS - LATE_ADDS:
                         add_bias(r, sums)
                     else:
                         last_sums.append((r, sums))

from contextlib import ExitStack

import concourse.masks as masks
import concourse.mybir as mybir

F32 = mybir.dt.float32
BF16 = mybir.dt.bfloat16
U32 = mybir.dt.uint32
U8 = mybir.dt.uint8
I32 = mybir.dt.int32
FP8X4 = mybir.dt.float8_e4m3fn_x4
ALU = mybir.AluOpType
ACT = mybir.ActivationFunctionType
AXIS = mybir.AxisListType

P = 128
BATCH = 4
TOKENS = 32
K = 1024
H = 1024
PACK = 4
K_PASS = P * PACK
PASSES = K // K_PASS
WORDS = K // 2
FLIPS = WORDS // P
BLOCKS = H // P
RUN = 2
RUNS = BLOCKS // RUN
COUPLING_ROUNDS = 2.0
HALF = H // 2
SQUARE = 32
CHUNK = H // SQUARE
IDLE_COLUMNS = 256
IDLE_START = 10
IDLE_HOLD = 3
LATE_ADDS = 2

FLOPS = 2 * P * K * H


def tile_dynamicroutingfusion_pa_s_kernel(tc, text_feat, vision_proj, Wt, bt, out_0, out_1):
    nc = tc.nc
    text_rows = text_feat.rearrange("b l k -> (b l) k")
    text_proj_out = out_0.rearrange("b l h -> (b l) h")
    weighted_out = out_1.rearrange("b l h -> (b l) h")

    with ExitStack() as ctx:
        ctx.enter_context(tc.manual_schedule())
        keep = ctx.enter_context(tc.tile_pool(name="keep", bufs=1))
        stage = ctx.enter_context(tc.tile_pool(name="stage", bufs=2 * RUN))
        flip_banks = ctx.enter_context(tc.psum_pool(name="flip_banks", bufs=4))
        sum_banks = ctx.enter_context(tc.psum_pool(name="sum_banks", bufs=4))

        x_rows = keep.tile([P, K], BF16)
        w_rows = keep.tile([P, BLOCKS, K], BF16)
        seed = keep.tile([P, 2, CHUNK], BF16, align_bytes=64)

        def load_blocks(first, count):
            nc.sync.dma_start(
                out=w_rows[:, first : first + count, :],
                in_=Wt[first * P : (first + count) * P, :].rearrange("(j p) k -> p j k", p=P),
            )

        nc.scalar.dma_start(out=seed[:, 0, :], in_=vision_proj.rearrange("b o (m e) -> (b o m) e", e=CHUNK))
        for b in range(BATCH):
            nc.scalar.dma_start(
                out=seed[b * SQUARE : (b + 1) * SQUARE, 1, :], in_=bt.rearrange("(m e) -> m e", e=CHUNK)
            )
        nc.sync.dma_start(out=x_rows[:], in_=text_rows)
        for first in range(0, BLOCKS - 2, 2):
            load_blocks(first, 2)
        load_blocks(BLOCKS - 2, 1)
        load_blocks(BLOCKS - 1, 1)

        identity = keep.tile([P, P], F32)
        masks.make_identity(nc, identity[:])
        table_warmer = keep.tile([P, 1], F32)
        nc.vector.memset(table_warmer[:], 0.0)
        nc.scalar.activation(out=table_warmer[:], in_=table_warmer[:], func=ACT.Exp)

        zeros = keep.tile([P, IDLE_COLUMNS * PACK], BF16, align_bytes=64)
        zero_codes = keep.tile([P, IDLE_COLUMNS], U32, align_bytes=64)
        zero_scales = keep.tile([P, IDLE_COLUMNS], U8, align_bytes=64)
        nc.vector.memset(zeros[:].bitcast(I32), 0)
        nc.vector.quantize_mx(out=zero_codes[:].bitcast(FP8X4), scales=zero_scales[:], in_=zeros[:])

        def idle_passes(count):
            unread = sum_banks.tile([P, IDLE_COLUMNS], F32, tag="sum_bank")
            for idle_pass in range(count):
                nc.tensor.matmul_mx(
                    out=unread[:],
                    lhsT=zero_codes[:, :P].bitcast(FP8X4),
                    lhsT_scale=zero_scales[:, :P],
                    rhs=zero_codes[:].bitcast(FP8X4),
                    rhs_scale=zero_scales[:],
                    start=True,
                    stop=True,
                )

        seed_flipped = keep.tile([P, SQUARE], F32, align_bytes=64)
        nc.vector.transpose(out=seed_flipped[:], in_=seed[:].rearrange("p w e -> p (w e)").bitcast(F32))
        seed_repeated = keep.tile([P, SQUARE, SQUARE], F32, align_bytes=64)
        nc.vector.tensor_copy(
            out=seed_repeated[:], in_=seed_flipped[:].unsqueeze(2).to_broadcast([P, SQUARE, SQUARE])
        )
        both_rows = keep.tile([P, SQUARE, 2, CHUNK], BF16, align_bytes=64)
        nc.vector.transpose(
            out=both_rows[:].rearrange("p m w e -> p (m w e)").bitcast(F32),
            in_=seed_repeated[:].rearrange("p m i -> p (m i)"),
        )
        vision_rows = both_rows[:, :, 0, :]
        bias_rows = both_rows[:, :, 1, :]

        def chunked(columns):
            return columns.rearrange("p (m e) -> p m e", e=CHUNK)

        x_codes = keep.tile([P, PASSES * P], U32, align_bytes=64)
        x_scales = keep.tile([P, PASSES * P], U8, align_bytes=64)
        w_codes = keep.tile([P, BLOCKS, PASSES * P], U32, align_bytes=64)
        w_scales = keep.tile([P, BLOCKS, PASSES * P], U8, align_bytes=64)

        def flip(rows):
            words = rows.bitcast(F32)
            bank = flip_banks.tile([P, FLIPS, P], F32)
            for j in range(FLIPS):
                nc.tensor.transpose(bank[:, j, :], words[:, j * P : (j + 1) * P], identity[:])
            grouped = stage.tile([P, PASSES * P * PACK], BF16, align_bytes=64)
            nc.scalar.copy(
                out=grouped[:].bitcast(F32).rearrange("p (g r u) -> p g r u", g=PASSES, u=2),
                in_=bank[:].rearrange("p (g u) r -> p g r u", u=2),
            )
            return grouped

        def quantise(grouped, codes, scales):
            nc.vector.quantize_mx(out=codes.bitcast(FP8X4), scales=scales, in_=grouped[:])

        text_proj = keep.tile([P, H], F32)
        products = keep.tile([P, H], F32)
        coupling_parts = keep.tile([P, BLOCKS], F32)

        def multiply(r):
            sums = sum_banks.tile([P, P], F32, tag="sum_bank")
            for g in range(PASSES):
                cols = slice(g * P, (g + 1) * P)
                nc.tensor.matmul_mx(
                    out=sums[:],
                    lhsT=x_codes[:, cols].bitcast(FP8X4),
                    lhsT_scale=x_scales[:, cols],
                    rhs=w_codes[:, r, cols].bitcast(FP8X4),
                    rhs_scale=w_scales[:, r, cols],
                    start=(g == 0),
                    stop=(g == PASSES - 1),
                )
            nc.vector.scalar_tensor_tensor(
                out=chunked(products[:, r * P : (r + 1) * P]),
                in0=chunked(sums[:]),
                scalar=COUPLING_ROUNDS,
                in1=vision_rows[:, r * P // CHUNK : (r + 1) * P // CHUNK, :],
                op0=ALU.mult,
                op1=ALU.mult,
                accum_out=coupling_parts[:, r : r + 1],
            )
            return sums

        def add_bias(r, sums):
            nc.vector.tensor_tensor(
                out=chunked(text_proj[:, r * P : (r + 1) * P]),
                in0=chunked(sums[:]),
                in1=bias_rows[:, r * P // CHUNK : (r + 1) * P // CHUNK, :],
                op=ALU.add,
            )

        idle_passes(IDLE_START)
        quantise(flip(x_rows[:]), x_codes[:], x_scales[:])
        idle_passes(IDLE_HOLD)
        last_sums = []
        for run in range(RUNS + 1):
            if run < RUNS:
                blocks = range(run * RUN, (run + 1) * RUN)
                flipped = [flip(w_rows[:, r, :]) for r in blocks]
                for r, grouped in zip(blocks, flipped):
                    quantise(grouped, w_codes[:, r, :], w_scales[:, r, :])
            if run == 0:
                idle_passes(IDLE_HOLD)
            if run >= 1:
                for r in range((run - 1) * RUN, run * RUN):
                    sums = multiply(r)
                    if run <= RUNS - LATE_ADDS:
                        add_bias(r, sums)
                    else:
                        last_sums.append((r, sums))
            if run * RUN == BLOCKS // 2:
                nc.sync.dma_start(out=text_proj_out[:, :HALF], in_=text_proj[:, :HALF])

        own_coupling = keep.tile([P, TOKENS], F32, align_bytes=64)
        nc.vector.tensor_reduce(
            out=own_coupling[:],
            in_=coupling_parts[:].unsqueeze(1).to_broadcast([P, TOKENS, BLOCKS]),
            axis=AXIS.X,
            op=ALU.add,
        )
        group_coupling = keep.tile([P, TOKENS], F32, align_bytes=64)
        nc.vector.transpose(out=group_coupling[:], in_=own_coupling[:])
        minus_max = keep.tile([P, 1], F32)
        nc.vector.tensor_reduce(
            out=minus_max[:], in_=group_coupling[:], axis=AXIS.X, op=ALU.max, negate=True
        )
        group_exp = keep.tile([P, TOKENS], F32)
        exp_sum = keep.tile([P, 1], F32)
        nc.scalar.activation(
            out=group_exp[:], in_=group_coupling[:], func=ACT.Exp, bias=minus_max[:], accum_out=exp_sum[:]
        )
        own_exp = keep.tile([P, 1], F32)
        nc.scalar.activation(out=own_exp[:], in_=own_coupling[:, 0:1], func=ACT.Exp, bias=minus_max[:])
        for r, sums in last_sums:
            add_bias(r, sums)
        nc.sync.dma_start(out=text_proj_out[:, HALF:], in_=text_proj[:, HALF:])
        one_over_sum = keep.tile([P, 1], F32)
        nc.vector.reciprocal(out=one_over_sum[:], in_=exp_sum[:])
        routing = keep.tile([P, 1], F32)
        nc.vector.tensor_tensor(out=routing[:], in0=own_exp[:], in1=one_over_sum[:], op=ALU.mult)

        weighted_left = keep.tile([P, HALF], F32)
        nc.vector.tensor_scalar(
            out=chunked(weighted_left[:]),
            in0=vision_rows[:, : HALF // CHUNK, :],
            scalar1=routing[:],
            scalar2=None,
            op0=ALU.mult,
        )
        nc.sync.dma_start(out=weighted_out[:, :HALF], in_=weighted_left[:])
        weighted_right = keep.tile([P, HALF], F32)
        nc.scalar.activation(
            out=chunked(weighted_right[:]), in_=vision_rows[:, HALF // CHUNK :, :], func=ACT.Copy, scale=routing[:]
        )
        nc.scalar.dma_start(out=weighted_out[:, HALF:], in_=weighted_right[:])
